import numpy as np
import ml_dtypes


def mxq(x, axis, fmt="e4m3"):
    dtype, down = {"e4m3": (ml_dtypes.float8_e4m3fn, 7), "e5m2": (ml_dtypes.float8_e5m2, 14)}[fmt]
    v = np.moveaxis(np.asarray(x, np.float32).astype(ml_dtypes.bfloat16).astype(np.float64), axis, -1)
    blocks = v.reshape(v.shape[:-1] + (-1, 32))
    amax = np.abs(blocks).max(-1, keepdims=True)
    byte = np.maximum(np.where(amax > 0, np.frexp(amax)[1] - 1 + 127, 0) - down, 1)
    scale = np.exp2(byte - 127.0)
    codes = (blocks / scale).astype(np.float32).astype(dtype).astype(np.float64)
    return np.moveaxis((codes * scale).reshape(v.shape), -1, axis)


WIDE = False


def mx_kscale(k):
    if not WIDE:
        return np.ones(k)
    levels = np.array([10, -10, 5, -5, 0])
    if k % 512:
        return np.exp2(np.random.permutation(np.resize(levels, k // 32))).repeat(32)
    a = np.empty((k // 512, 16))
    for p in range(k // 512):
        a[p, :8] = np.random.permutation(np.resize(levels, 8))
        for g in range(8):
            far = levels[np.abs(levels - a[p, g]) >= 10]
            a[p, g + 8] = far[np.random.randint(len(far))]
    return np.exp2(a.ravel()).repeat(32)


BF16 = ml_dtypes.bfloat16


def bf(x):
    return np.asarray(x, np.float32).astype(BF16)


def f64(x):
    return np.asarray(x).astype(np.float64)


B, SQ, SK, D, DK, L = 2, 8192, 256, 512, 64, 10000
P = max(SQ, SK)


def setup_inputs():
    s, t = mx_kscale(D), mx_kscale(D)
    return {"pe": bf(np.random.standard_normal((P, D)) * s),
            "Uq": bf(np.random.standard_normal((D, D)) * 0.6 / np.sqrt(D) / s[:, None] * t),
            "Uk": bf(np.random.standard_normal((D, D)) * 0.6 / np.sqrt(D) / s[:, None] / t)}


def reference(pe, Uq, Uk):
    peq = mxq(f64(pe), 1, "e4m3")
    q_pe = peq[:SQ] @ mxq(f64(Uq), 0, "e4m3")
    k_pe = peq[:SK] @ mxq(f64(Uk), 0, "e4m3")
    return mxq(q_pe, 1, "e4m3") @ mxq(k_pe, 1, "e4m3").T

@@ -1,0 +1,190 @@
+from contextlib import ExitStack
+
+import concourse.masks as masks
+import concourse.mybir as mybir
+
+BF16 = mybir.dt.bfloat16
+F32 = mybir.dt.float32
+U32 = mybir.dt.uint32
+U8 = mybir.dt.uint8
+FP8X4 = mybir.dt.float8_e4m3fn_x4
+
+P = 128
+PACK = 4
+SQ, SK, D = 8192, 256, 512
+BANK = 512
+
+CHUNK_ROWS = 4
+KEY_ROWS = SK // P
+CHUNK = CHUNK_ROWS * P
+N_CHUNKS = SQ // CHUNK
+
+KEYS = 0
+N_JOBS = N_CHUNKS + 1
+
+PROJECT_LAG = 1
+REQUANTISE_LAG = 2
+SCORE_LAG = 3
+
+FLOPS = 2 * D * (SQ * D + SK * D + SQ * SK)
+
+
+def tile_multiheadattention_tupe_pa_t_kernel(tc, pe, Uq, Uk, out):
+    nc = tc.nc
+    with ExitStack() as ctx:
+        keep = ctx.enter_context(tc.tile_pool(name="keep", bufs=1))
+        rows_in = ctx.enter_context(tc.tile_pool(name="rows_in", bufs=N_CHUNKS))
+        work = ctx.enter_context(tc.tile_pool(name="work", bufs=3))
+        rows_out = ctx.enter_context(tc.tile_pool(name="rows_out", bufs=8))
+        psum_x = ctx.enter_context(tc.psum_pool(name="psum_x", bufs=2))
+        psum_y = ctx.enter_context(tc.psum_pool(name="psum_y", bufs=4))
+        psum_s = ctx.enter_context(tc.psum_pool(name="psum_s", bufs=2))
+        ctx.enter_context(tc.manual_schedule())
+
+        def job_rows(job):
+            return KEY_ROWS if job == KEYS else CHUNK_ROWS
+
+        def empty_bank(job, bank, out_ap, in_ap):
+            if bank == 0 and job != KEYS:
+                nc.vector.tensor_copy(out=out_ap, in_=in_ap)
+            else:
+                nc.scalar.copy(out=out_ap, in_=in_ap)
+
+        def quantise(grouped, pool, tag):
+            width = grouped.shape[1] // PACK
+            codes = pool.tile([P, width], U32, tag=tag + "_codes", align_bytes=64)
+            scales = pool.tile([P, width], U8, tag=tag + "_scales", align_bytes=64)
+            nc.vector.quantize_mx(out=codes[:].bitcast(FP8X4), scales=scales[:], in_=grouped[:])
+            return codes, scales
+
+        def load_weights(w, tag):
+            raw = keep.tile([P, PACK, D], BF16, tag=tag + "_raw")
+            nc.sync.dma_start(out=raw[:], in_=w.rearrange("(q t) c -> q t c", t=PACK))
+            return raw
+
+        uq_raw = load_weights(Uq, "uq")
+        uk_raw = load_weights(Uk, "uk")
+        pe_rows = {}
+        key_rows = keep.tile([P, KEY_ROWS * D], BF16, tag="key_rows")
+        nc.sync.dma_start(
+            out=key_rows[:].rearrange("p (r d) -> p r d", r=KEY_ROWS),
+            in_=pe[0:SK, :].rearrange("(r p) d -> p r d", p=P),
+        )
+        pe_rows[KEYS] = key_rows
+        for job in range(1, N_JOBS):
+            first = (job - 1) * CHUNK
+            chunk_rows = rows_in.tile([P, CHUNK_ROWS * D], BF16, tag="chunk_rows")
+            nc.sync.dma_start(
+                out=chunk_rows[:],
+                in_=pe[first : first + CHUNK, :].rearrange("(p r) d -> p (r d)", r=CHUNK_ROWS),
+            )
+            pe_rows[job] = chunk_rows
+
+        identity = keep.tile([P, P], F32, tag="identity")
+        masks.make_identity(nc, identity[:])
+
+        def regroup_weights(raw, tag):
+            grouped = keep.tile([P, PACK * D], BF16, tag=tag + "_grouped", align_bytes=64)
+            dst = grouped[:].rearrange("q (f m t) -> q m t f", f=PACK, t=PACK)
+            src = raw[:].rearrange("q t (m f) -> q m t f", f=PACK)
+            half = P // 2
+            nc.vector.tensor_copy(out=dst[:, :half], in_=src[:, :half])
+            nc.scalar.copy(out=dst[:, half:], in_=src[:, half:])
+            return grouped
+
+        uq_grouped = regroup_weights(uq_raw, "uq")
+        uk_grouped = regroup_weights(uk_raw, "uk")
+        uq_mx = quantise(uq_grouped, keep, "uq")
+        uk_mx = quantise(uk_grouped, keep, "uk")
+
+        x_grouped, x_mx, y_grouped, y_mx = {}, {}, {}, {}
+
+        def transpose_features(job):
+            words = pe_rows[job][:].bitcast(F32)
+            grouped = work.tile([P, job_rows(job) * P * PACK], BF16, tag="x_grouped", align_bytes=64)
+            grouped_words = grouped[:].bitcast(F32)
+            for bank in range(job_rows(job) // 2):
+                xt = psum_x.tile([P, 2, 2 * P], F32, tag="xt")
+                for r in range(2):
+                    for u in range(2):
+                        row = (2 * bank + r) * 2 * P
+                        nc.tensor.transpose(
+                            xt[:, u, r * P : (r + 1) * P],
+                            words[:, row + u : row + 2 * P : 2],
+                            identity[:],
+                        )
+                empty_bank(
+                    job,
+                    bank,
+                    grouped_words[:, bank * BANK : (bank + 1) * BANK].rearrange(
+                        "q (w u) -> q w u", u=2
+                    ),
+                    xt[:].rearrange("q u w -> q w u"),
+                )
+            x_grouped[job] = grouped
+
+        def project(job):
+            w_codes, w_scales = uk_mx if job == KEYS else uq_mx
+            x_codes, x_scales = x_mx[job]
+            grouped = work.tile([P, job_rows(job) * P * PACK], BF16, tag="y_grouped", align_bytes=64)
+            for bank in range(job_rows(job)):
+                cols = slice(bank * P, (bank + 1) * P)
+                yt = psum_y.tile([P, PACK, P], F32, tag="yt")
+                for f in range(PACK):
+                    feats = slice(f * P, (f + 1) * P)
+                    nc.tensor.matmul_mx(
+                        out=yt[:, f, :],
+                        lhsT=w_codes[:, feats].bitcast(FP8X4),
+                        lhsT_scale=w_scales[:, feats],
+                        rhs=x_codes[:, cols].bitcast(FP8X4),
+                        rhs_scale=x_scales[:, cols],
+                        start=True,
+                        stop=True,
+                    )
+                empty_bank(
+                    job,
+                    bank,
+                    grouped[:, bank * BANK : (bank + 1) * BANK].rearrange(
+                        "m (w f) -> m w f", f=PACK
+                    ),
+                    yt[:].rearrange("m f w -> m w f"),
+                )
+            y_grouped[job] = grouped
+
+        def score(job):
+            q_codes, q_scales = y_mx[job]
+            k_codes, k_scales = y_mx[KEYS]
+            first = (job - 1) * CHUNK
+            out_rows = out[first : first + CHUNK, :].rearrange(
+                "(p b r) n -> p b (r n)", b=CHUNK_ROWS // 2, r=2
+            )
+            for bank in range(CHUNK_ROWS // 2):
+                st = psum_s.tile([P, 2, SK], F32, tag="st")
+                for r in range(2):
+                    cols = slice((2 * bank + r) * P, (2 * bank + r + 1) * P)
+                    nc.tensor.matmul_mx(
+                        out=st[:, r, :],
+                        lhsT=q_codes[:, cols].bitcast(FP8X4),
+                        lhsT_scale=q_scales[:, cols],
+                        rhs=k_codes[:].bitcast(FP8X4),
+                        rhs_scale=k_scales[:],
+                        start=True,
+                        stop=True,
+                    )
+                result = rows_out.tile([P, BANK], F32, tag="result")
+                empty_bank(job, bank, result[:], st[:].rearrange("p r n -> p (r n)"))
+                nc.sync.dma_start(out=out_rows[:, bank, :], in_=result[:])
+
+        for step in range(N_JOBS + SCORE_LAG):
+            if step < N_JOBS:
+                transpose_features(step)
+            if KEYS < step - SCORE_LAG < N_JOBS:
+                score(step - SCORE_LAG)
+            if step - REQUANTISE_LAG == KEYS:
+                y_mx[KEYS] = quantise(y_grouped[KEYS], keep, "k")
+            if KEYS < step - REQUANTISE_LAG < N_JOBS:
+                y_mx[step - REQUANTISE_LAG] = quantise(y_grouped[step - REQUANTISE_LAG], work, "q")
+            if 0 <= step - PROJECT_LAG < N_JOBS:
+                project(step - PROJECT_LAG)
+            if step < N_JOBS:
+                x_mx[step] = quantise(x_grouped[step], work, "x")

@@ -15,16 +15,18 @@ SQ, SK, D = 8192, 256, 512
 BANK = 512
 
 CHUNK_ROWS = 4
-KEY_ROWS = SK // P
 CHUNK = CHUNK_ROWS * P
 N_CHUNKS = SQ // CHUNK
-
-KEYS = 0
-N_JOBS = N_CHUNKS + 1
+LAST = N_CHUNKS - 1
+KEY_ROWS = SK // P
 
 PROJECT_LAG = 1
 REQUANTISE_LAG = 2
-SCORE_LAG = 3
+SCORE_LAG = 4
+
+RELIEF = 4
+
+VECTOR_COLUMNS = 80
 
 FLOPS = 2 * D * (SQ * D + SK * D + SQ * SK)
 
@@ -34,18 +36,15 @@ def tile_multiheadattention_tupe_pa_t_kernel(tc, pe, Uq, Uk, out):
     with ExitStack() as ctx:
         keep = ctx.enter_context(tc.tile_pool(name="keep", bufs=1))
         rows_in = ctx.enter_context(tc.tile_pool(name="rows_in", bufs=N_CHUNKS))
-        work = ctx.enter_context(tc.tile_pool(name="work", bufs=3))
+        work = ctx.enter_context(tc.tile_pool(name="work", bufs=4))
         rows_out = ctx.enter_context(tc.tile_pool(name="rows_out", bufs=8))
         psum_x = ctx.enter_context(tc.psum_pool(name="psum_x", bufs=2))
         psum_y = ctx.enter_context(tc.psum_pool(name="psum_y", bufs=4))
         psum_s = ctx.enter_context(tc.psum_pool(name="psum_s", bufs=2))
         ctx.enter_context(tc.manual_schedule())
 
-        def job_rows(job):
-            return KEY_ROWS if job == KEYS else CHUNK_ROWS
-
-        def empty_bank(job, bank, out_ap, in_ap):
-            if bank == 0 and job != KEYS:
+        def empty_bank(on_vector, out_ap, in_ap):
+            if on_vector:
                 nc.vector.tensor_copy(out=out_ap, in_=in_ap)
             else:
                 nc.scalar.copy(out=out_ap, in_=in_ap)
@@ -54,7 +53,7 @@ def tile_multiheadattention_tupe_pa_t_kernel(tc, pe, Uq, Uk, out):
             width = grouped.shape[1] // PACK
             codes = pool.tile([P, width], U32, tag=tag + "_codes", align_bytes=64)
             scales = pool.tile([P, width], U8, tag=tag + "_scales", align_bytes=64)
-            nc.vector.quantize_mx(out=codes[:].bitcast(FP8X4), scales=scales[:], in_=grouped[:])
+            nc.vector.quantize_mx(out=codes[:].bitcast(FP8X4), scales=scales[:], in_=grouped)
             return codes, scales
 
         def load_weights(w, tag):
@@ -62,23 +61,22 @@ def tile_multiheadattention_tupe_pa_t_kernel(tc, pe, Uq, Uk, out):
             nc.sync.dma_start(out=raw[:], in_=w.rearrange("(q t) c -> q t c", t=PACK))
             return raw
 
+        def chunk_view(tensor, chunk):
+            rows = tensor[chunk * CHUNK : (chunk + 1) * CHUNK, :]
+            if chunk == 0:
+                return rows.rearrange("(r p) c -> p r c", p=P)
+            return rows.rearrange("(p r) c -> p r c", r=CHUNK_ROWS)
+
+        def load_chunk(chunk):
+            chunk_rows = rows_in.tile([P, CHUNK_ROWS, D], BF16, tag="chunk_rows")
+            nc.sync.dma_start(out=chunk_rows[:], in_=chunk_view(pe, chunk))
+            return chunk_rows
+
         uq_raw = load_weights(Uq, "uq")
+        pe_rows = [load_chunk(0), load_chunk(1)]
         uk_raw = load_weights(Uk, "uk")
-        pe_rows = {}
-        key_rows = keep.tile([P, KEY_ROWS * D], BF16, tag="key_rows")
-        nc.sync.dma_start(
-            out=key_rows[:].rearrange("p (r d) -> p r d", r=KEY_ROWS),
-            in_=pe[0:SK, :].rearrange("(r p) d -> p r d", p=P),
-        )
-        pe_rows[KEYS] = key_rows
-        for job in range(1, N_JOBS):
-            first = (job - 1) * CHUNK
-            chunk_rows = rows_in.tile([P, CHUNK_ROWS * D], BF16, tag="chunk_rows")
-            nc.sync.dma_start(
-                out=chunk_rows[:],
-                in_=pe[first : first + CHUNK, :].rearrange("(p r) d -> p (r d)", r=CHUNK_ROWS),
-            )
-            pe_rows[job] = chunk_rows
+        for chunk in range(2, N_CHUNKS):
+            pe_rows.append(load_chunk(chunk))
 
         identity = keep.tile([P, P], F32, tag="identity")
         masks.make_identity(nc, identity[:])
@@ -87,23 +85,21 @@ def tile_multiheadattention_tupe_pa_t_kernel(tc, pe, Uq, Uk, out):
             grouped = keep.tile([P, PACK * D], BF16, tag=tag + "_grouped", align_bytes=64)
             dst = grouped[:].rearrange("q (f m t) -> q m t f", f=PACK, t=PACK)
             src = raw[:].rearrange("q t (m f) -> q m t f", f=PACK)
-            half = P // 2
-            nc.vector.tensor_copy(out=dst[:, :half], in_=src[:, :half])
-            nc.scalar.copy(out=dst[:, half:], in_=src[:, half:])
+            cut = VECTOR_COLUMNS
+            nc.vector.tensor_copy(out=dst[:, :cut], in_=src[:, :cut])
+            nc.scalar.copy(out=dst[:, cut:], in_=src[:, cut:])
             return grouped
 
         uq_grouped = regroup_weights(uq_raw, "uq")
-        uk_grouped = regroup_weights(uk_raw, "uk")
-        uq_mx = quantise(uq_grouped, keep, "uq")
-        uk_mx = quantise(uk_grouped, keep, "uk")
+        uq_mx = quantise(uq_grouped[:], keep, "uq")
 
         x_grouped, x_mx, y_grouped, y_mx = {}, {}, {}, {}
 
-        def transpose_features(job):
-            words = pe_rows[job][:].bitcast(F32)
-            grouped = work.tile([P, job_rows(job) * P * PACK], BF16, tag="x_grouped", align_bytes=64)
+        def transpose_features(chunk):
+            words = pe_rows[chunk][:].rearrange("p r d -> p (r d)").bitcast(F32)
+            grouped = work.tile([P, CHUNK * PACK], BF16, tag="x_grouped", align_bytes=64)
             grouped_words = grouped[:].bitcast(F32)
-            for bank in range(job_rows(job) // 2):
+            for bank in range(CHUNK_ROWS // 2):
                 xt = psum_x.tile([P, 2, 2 * P], F32, tag="xt")
                 for r in range(2):
                     for u in range(2):
@@ -114,20 +110,19 @@ def tile_multiheadattention_tupe_pa_t_kernel(tc, pe, Uq, Uk, out):
                             identity[:],
                         )
                 empty_bank(
-                    job,
-                    bank,
+                    bank == 0,
                     grouped_words[:, bank * BANK : (bank + 1) * BANK].rearrange(
                         "q (w u) -> q w u", u=2
                     ),
                     xt[:].rearrange("q u w -> q w u"),
                 )
-            x_grouped[job] = grouped
+            x_grouped[chunk] = grouped
 
-        def project(job):
-            w_codes, w_scales = uk_mx if job == KEYS else uq_mx
-            x_codes, x_scales = x_mx[job]
-            grouped = work.tile([P, job_rows(job) * P * PACK], BF16, tag="y_grouped", align_bytes=64)
-            for bank in range(job_rows(job)):
+        def project(x_operand, w_operand, rows, vector_banks):
+            w_codes, w_scales = w_operand
+            x_codes, x_scales = x_operand
+            grouped = work.tile([P, CHUNK * PACK], BF16, tag="y_grouped", align_bytes=64)
+            for bank in range(rows):
                 cols = slice(bank * P, (bank + 1) * P)
                 yt = psum_y.tile([P, PACK, P], F32, tag="yt")
                 for f in range(PACK):
@@ -142,26 +137,46 @@ def tile_multiheadattention_tupe_pa_t_kernel(tc, pe, Uq, Uk, out):
                         stop=True,
                     )
                 empty_bank(
-                    job,
-                    bank,
+                    bank in vector_banks,
                     grouped[:, bank * BANK : (bank + 1) * BANK].rearrange(
                         "m (w f) -> m w f", f=PACK
                     ),
                     yt[:].rearrange("m f w -> m w f"),
                 )
-            y_grouped[job] = grouped
+            return grouped
 
-        def score(job):
-            q_codes, q_scales = y_mx[job]
-            k_codes, k_scales = y_mx[KEYS]
-            first = (job - 1) * CHUNK
-            out_rows = out[first : first + CHUNK, :].rearrange(
-                "(p b r) n -> p b (r n)", b=CHUNK_ROWS // 2, r=2
-            )
+        def project_queries(chunk):
+            if chunk == LAST:
+                vector_banks = (0, 2)
+            elif chunk % RELIEF == RELIEF - 1:
+                vector_banks = ()
+            else:
+                vector_banks = (0,)
+            y_grouped[chunk] = project(x_mx[chunk], uq_mx, CHUNK_ROWS, vector_banks)
+
+        def requantise(chunk):
+            grouped = y_grouped[chunk][:]
+            half = CHUNK * PACK // 2
+            if chunk == LAST:
+                y_mx[chunk] = [
+                    [t[:] for t in quantise(grouped[:, h * half : (h + 1) * half], keep, "q%d" % h)]
+                    for h in range(2)
+                ]
+            else:
+                codes, scales = quantise(grouped, work, "q")
+                width = CHUNK // 2
+                y_mx[chunk] = [
+                    [t[:, h * width : (h + 1) * width] for t in (codes, scales)] for h in range(2)
+                ]
+
+        def score(chunk, k_operand):
+            k_codes, k_scales = k_operand
+            out_rows = chunk_view(out, chunk)
             for bank in range(CHUNK_ROWS // 2):
+                q_codes, q_scales = y_mx[chunk][bank]
                 st = psum_s.tile([P, 2, SK], F32, tag="st")
                 for r in range(2):
-                    cols = slice((2 * bank + r) * P, (2 * bank + r + 1) * P)
+                    cols = slice(r * P, (r + 1) * P)
                     nc.tensor.matmul_mx(
                         out=st[:, r, :],
                         lhsT=q_codes[:, cols].bitcast(FP8X4),
@@ -171,20 +186,27 @@ def tile_multiheadattention_tupe_pa_t_kernel(tc, pe, Uq, Uk, out):
                         start=True,
                         stop=True,
                     )
-                result = rows_out.tile([P, BANK], F32, tag="result")
-                empty_bank(job, bank, result[:], st[:].rearrange("p r n -> p (r n)"))
-                nc.sync.dma_start(out=out_rows[:, bank, :], in_=result[:])
+                result = rows_out.tile([P, 2, SK], F32, tag="result")
+                empty_bank(bank == 0, result[:], st[:])
+                nc.sync.dma_start(out=out_rows[:, 2 * bank : 2 * bank + 2, :], in_=result[:])
 
-        for step in range(N_JOBS + SCORE_LAG):
-            if step < N_JOBS:
+        KEY_STEP = 1 + PROJECT_LAG
+        for step in range(N_CHUNKS + SCORE_LAG):
+            if step < N_CHUNKS:
                 transpose_features(step)
-            if KEYS < step - SCORE_LAG < N_JOBS:
-                score(step - SCORE_LAG)
-            if step - REQUANTISE_LAG == KEYS:
-                y_mx[KEYS] = quantise(y_grouped[KEYS], keep, "k")
-            if KEYS < step - REQUANTISE_LAG < N_JOBS:
-                y_mx[step - REQUANTISE_LAG] = quantise(y_grouped[step - REQUANTISE_LAG], work, "q")
-            if 0 <= step - PROJECT_LAG < N_JOBS:
-                project(step - PROJECT_LAG)
-            if step < N_JOBS:
-                x_mx[step] = quantise(x_grouped[step], work, "x")
+            if 0 <= step - SCORE_LAG:
+                score(step - SCORE_LAG, k_mx)
+            if 0 <= step - PROJECT_LAG < N_CHUNKS:
+                project_queries(step - PROJECT_LAG)
+            if step == KEY_STEP:
+                k_grouped = project(x_mx[0], uk_mx, KEY_ROWS, ())
+            if step == KEY_STEP + 1:
+                k_mx = quantise(k_grouped[:, : KEY_ROWS * BANK], keep, "k")
+            if 0 <= step - REQUANTISE_LAG < N_CHUNKS:
+                requantise(step - REQUANTISE_LAG)
+            if step < N_CHUNKS:
+                x_mx[step] = quantise(x_grouped[step][:], work, "x")
+            if step == 0:
+                uk_grouped = regroup_weights(uk_raw, "uk")
+            if step == KEY_STEP - 1:
+                uk_mx = quantise(uk_grouped[:], keep, "uk")

@@ -38,9 +38,7 @@ def tile_multiheadattention_tupe_pa_t_kernel(tc, pe, Uq, Uk, out):
         rows_in = ctx.enter_context(tc.tile_pool(name="rows_in", bufs=N_CHUNKS))
         work = ctx.enter_context(tc.tile_pool(name="work", bufs=4))
         rows_out = ctx.enter_context(tc.tile_pool(name="rows_out", bufs=8))
-        psum_x = ctx.enter_context(tc.psum_pool(name="psum_x", bufs=2))
-        psum_y = ctx.enter_context(tc.psum_pool(name="psum_y", bufs=4))
-        psum_s = ctx.enter_context(tc.psum_pool(name="psum_s", bufs=2))
+        psum = ctx.enter_context(tc.psum_pool(name="psum", bufs=8))
         ctx.enter_context(tc.manual_schedule())
 
         def empty_bank(on_vector, out_ap, in_ap):
@@ -100,7 +98,7 @@ def tile_multiheadattention_tupe_pa_t_kernel(tc, pe, Uq, Uk, out):
             grouped = work.tile([P, CHUNK * PACK], BF16, tag="x_grouped", align_bytes=64)
             grouped_words = grouped[:].bitcast(F32)
             for bank in range(CHUNK_ROWS // 2):
-                xt = psum_x.tile([P, 2, 2 * P], F32, tag="xt")
+                xt = psum.tile([P, 2, 2 * P], F32, tag="bank")
                 for r in range(2):
                     for u in range(2):
                         row = (2 * bank + r) * 2 * P
@@ -124,7 +122,7 @@ def tile_multiheadattention_tupe_pa_t_kernel(tc, pe, Uq, Uk, out):
             grouped = work.tile([P, CHUNK * PACK], BF16, tag="y_grouped", align_bytes=64)
             for bank in range(rows):
                 cols = slice(bank * P, (bank + 1) * P)
-                yt = psum_y.tile([P, PACK, P], F32, tag="yt")
+                yt = psum.tile([P, PACK, P], F32, tag="bank")
                 for f in range(PACK):
                     feats = slice(f * P, (f + 1) * P)
                     nc.tensor.matmul_mx(
@@ -174,7 +172,7 @@ def tile_multiheadattention_tupe_pa_t_kernel(tc, pe, Uq, Uk, out):
             out_rows = chunk_view(out, chunk)
             for bank in range(CHUNK_ROWS // 2):
                 q_codes, q_scales = y_mx[chunk][bank]
-                st = psum_s.tile([P, 2, SK], F32, tag="st")
+                st = psum.tile([P, 2, SK], F32, tag="bank")
                 for r in range(2):
                     cols = slice(r * P, (r + 1) * P)
                     nc.tensor.matmul_mx(

@@ -24,7 +24,9 @@ PROJECT_LAG = 1
 REQUANTISE_LAG = 2
 SCORE_LAG = 4
 
-RELIEF = 4
+RELIEF = 5
+
+WARM_UP = (5, 2, 1)
 
 VECTOR_COLUMNS = 80
 
@@ -67,11 +69,15 @@ def tile_multiheadattention_tupe_pa_t_kernel(tc, pe, Uq, Uk, out):
 
         def load_chunk(chunk):
             chunk_rows = rows_in.tile([P, CHUNK_ROWS, D], BF16, tag="chunk_rows")
-            nc.sync.dma_start(out=chunk_rows[:], in_=chunk_view(pe, chunk))
+            view = chunk_view(pe, chunk)
+            rows = CHUNK_ROWS // 2 if chunk == 0 else CHUNK_ROWS
+            for r in range(0, CHUNK_ROWS, rows):
+                nc.sync.dma_start(out=chunk_rows[:, r : r + rows, :], in_=view[:, r : r + rows, :])
             return chunk_rows
 
+        pe_rows = [load_chunk(0)]
         uq_raw = load_weights(Uq, "uq")
-        pe_rows = [load_chunk(0), load_chunk(1)]
+        pe_rows.append(load_chunk(1))
         uk_raw = load_weights(Uk, "uk")
         for chunk in range(2, N_CHUNKS):
             pe_rows.append(load_chunk(chunk))
@@ -88,10 +94,15 @@ def tile_multiheadattention_tupe_pa_t_kernel(tc, pe, Uq, Uk, out):
             nc.scalar.copy(out=dst[:, cut:], in_=src[:, cut:])
             return grouped
 
-        uq_grouped = regroup_weights(uq_raw, "uq")
-        uq_mx = quantise(uq_grouped[:], keep, "uq")
-
         x_grouped, x_mx, y_grouped, y_mx = {}, {}, {}, {}
+
+        zeros = keep.tile([P, BANK], BF16, tag="zeros")
+        nc.vector.memset(zeros[:], 0.0)
+
+        def warm_up(count):
+            idle = psum.tile([P, BANK], F32, tag="bank")
+            for i in range(count):
+                nc.tensor.matmul(idle[:], lhsT=zeros[:, :P], rhs=zeros[:], start=True, stop=True)
 
         def transpose_features(chunk):
             words = pe_rows[chunk][:].rearrange("p r d -> p (r d)").bitcast(F32)
@@ -108,7 +119,7 @@ def tile_multiheadattention_tupe_pa_t_kernel(tc, pe, Uq, Uk, out):
                             identity[:],
                         )
                 empty_bank(
-                    bank == 0,
+                    bank == (1 if chunk == 0 else 0),
                     grouped_words[:, bank * BANK : (bank + 1) * BANK].rearrange(
                         "q (w u) -> q w u", u=2
                     ),
@@ -189,9 +200,14 @@ def tile_multiheadattention_tupe_pa_t_kernel(tc, pe, Uq, Uk, out):
                 nc.sync.dma_start(out=out_rows[:, 2 * bank : 2 * bank + 2, :], in_=result[:])
 
         KEY_STEP = 1 + PROJECT_LAG
+        warm_up(WARM_UP[0])
         for step in range(N_CHUNKS + SCORE_LAG):
             if step < N_CHUNKS:
                 transpose_features(step)
+            if step < 2:
+                warm_up(WARM_UP[1 + step])
+            if step == 0:
+                uq_grouped = regroup_weights(uq_raw, "uq")
             if 0 <= step - SCORE_LAG:
                 score(step - SCORE_LAG, k_mx)
             if 0 <= step - PROJECT_LAG < N_CHUNKS:
@@ -205,6 +221,7 @@ def tile_multiheadattention_tupe_pa_t_kernel(tc, pe, Uq, Uk, out):
             if step < N_CHUNKS:
                 x_mx[step] = quantise(x_grouped[step][:], work, "x")
             if step == 0:
+                uq_mx = quantise(uq_grouped[:], keep, "uq")
                 uk_grouped = regroup_weights(uk_raw, "uk")
             if step == KEY_STEP - 1:
                 uk_mx = quantise(uk_grouped[:], keep, "uk")

@@ -28,7 +28,8 @@ RELIEF = 5
 
 WARM_UP = (5, 2, 1)
 
-VECTOR_COLUMNS = 80
+UQ_COLUMNS = (0, 80, 48)
+UK_COLUMNS = (80, 24, 24)
 
 FLOPS = 2 * D * (SQ * D + SK * D + SQ * SK)
 
@@ -75,9 +76,8 @@ def tile_multiheadattention_tupe_pa_t_kernel(tc, pe, Uq, Uk, out):
                 nc.sync.dma_start(out=chunk_rows[:, r : r + rows, :], in_=view[:, r : r + rows, :])
             return chunk_rows
 
-        pe_rows = [load_chunk(0)]
         uq_raw = load_weights(Uq, "uq")
-        pe_rows.append(load_chunk(1))
+        pe_rows = [load_chunk(0), load_chunk(1)]
         uk_raw = load_weights(Uk, "uk")
         for chunk in range(2, N_CHUNKS):
             pe_rows.append(load_chunk(chunk))
@@ -85,13 +85,22 @@ def tile_multiheadattention_tupe_pa_t_kernel(tc, pe, Uq, Uk, out):
         identity = keep.tile([P, P], F32, tag="identity")
         masks.make_identity(nc, identity[:])
 
-        def regroup_weights(raw, tag):
+        def regroup_weights(raw, tag, columns):
             grouped = keep.tile([P, PACK * D], BF16, tag=tag + "_grouped", align_bytes=64)
             dst = grouped[:].rearrange("q (f m t) -> q m t f", f=PACK, t=PACK)
             src = raw[:].rearrange("q t (m f) -> q m t f", f=PACK)
-            cut = VECTOR_COLUMNS
-            nc.vector.tensor_copy(out=dst[:, :cut], in_=src[:, :cut])
-            nc.scalar.copy(out=dst[:, cut:], in_=src[:, cut:])
+            a, b = columns[0], columns[0] + columns[1]
+            if a:
+                nc.gpsimd.tensor_scalar(
+                    out=dst[:, :a],
+                    in0=src[:, :a],
+                    scalar1=1.0,
+                    scalar2=0.0,
+                    op0=mybir.AluOpType.mult,
+                    op1=mybir.AluOpType.add,
+                )
+            nc.vector.tensor_copy(out=dst[:, a:b], in_=src[:, a:b])
+            nc.scalar.copy(out=dst[:, b:], in_=src[:, b:])
             return grouped
 
         x_grouped, x_mx, y_grouped, y_mx = {}, {}, {}, {}
@@ -181,13 +190,15 @@ def tile_multiheadattention_tupe_pa_t_kernel(tc, pe, Uq, Uk, out):
         def score(chunk, k_operand):
             k_codes, k_scales = k_operand
             out_rows = chunk_view(out, chunk)
-            for bank in range(CHUNK_ROWS // 2):
-                q_codes, q_scales = y_mx[chunk][bank]
-                st = psum.tile([P, 2, SK], F32, tag="bank")
-                for r in range(2):
+            bank_rows = 1 if chunk == LAST else 2
+            for bank in range(CHUNK_ROWS // bank_rows):
+                st = psum.tile([P, bank_rows, SK], F32, tag="bank")
+                for i in range(bank_rows):
+                    half, r = divmod(bank * bank_rows + i, 2)
+                    q_codes, q_scales = y_mx[chunk][half]
                     cols = slice(r * P, (r + 1) * P)
                     nc.tensor.matmul_mx(
-                        out=st[:, r, :],
+                        out=st[:, i, :],
                         lhsT=q_codes[:, cols].bitcast(FP8X4),
                         lhsT_scale=q_scales[:, cols],
                         rhs=k_codes[:].bitcast(FP8X4),
@@ -195,19 +206,20 @@ def tile_multiheadattention_tupe_pa_t_kernel(tc, pe, Uq, Uk, out):
                         start=True,
                         stop=True,
                     )
-                result = rows_out.tile([P, 2, SK], F32, tag="result")
-                empty_bank(bank == 0, result[:], st[:])
-                nc.sync.dma_start(out=out_rows[:, 2 * bank : 2 * bank + 2, :], in_=result[:])
+                result = rows_out.tile([P, bank_rows, SK], F32, tag="result")
+                empty_bank(bank % 2 == 0, result[:], st[:])
+                rows = slice(bank * bank_rows, (bank + 1) * bank_rows)
+                nc.sync.dma_start(out=out_rows[:, rows, :], in_=result[:])
 
         KEY_STEP = 1 + PROJECT_LAG
+        uq_grouped = regroup_weights(uq_raw, "uq", UQ_COLUMNS)
+        uq_mx = quantise(uq_grouped[:], keep, "uq")
         warm_up(WARM_UP[0])
         for step in range(N_CHUNKS + SCORE_LAG):
             if step < N_CHUNKS:
                 transpose_features(step)
             if step < 2:
                 warm_up(WARM_UP[1 + step])
-            if step == 0:
-                uq_grouped = regroup_weights(uq_raw, "uq")
             if 0 <= step - SCORE_LAG:
                 score(step - SCORE_LAG, k_mx)
             if 0 <= step - PROJECT_LAG < N_CHUNKS:
@@ -221,7 +233,6 @@ def tile_multiheadattention_tupe_pa_t_kernel(tc, pe, Uq, Uk, out):
             if step < N_CHUNKS:
                 x_mx[step] = quantise(x_grouped[step][:], work, "x")
             if step == 0:
-                uq_mx = quantise(uq_grouped[:], keep, "uq")
-                uk_grouped = regroup_weights(uk_raw, "uk")
+                uk_grouped = regroup_weights(uk_raw, "uk", UK_COLUMNS)
             if step == KEY_STEP - 1:
                 uk_mx = quantise(uk_grouped[:], keep, "uk")

@@ -40,7 +40,7 @@ def tile_multiheadattention_tupe_pa_t_kernel(tc, pe, Uq, Uk, out):
         keep = ctx.enter_context(tc.tile_pool(name="keep", bufs=1))
         rows_in = ctx.enter_context(tc.tile_pool(name="rows_in", bufs=N_CHUNKS))
         work = ctx.enter_context(tc.tile_pool(name="work", bufs=4))
-        rows_out = ctx.enter_context(tc.tile_pool(name="rows_out", bufs=8))
+        rows_out = ctx.enter_context(tc.tile_pool(name="rows_out", bufs=16))
         psum = ctx.enter_context(tc.psum_pool(name="psum", bufs=8))
         ctx.enter_context(tc.manual_schedule())
 
@@ -228,10 +228,10 @@ def tile_multiheadattention_tupe_pa_t_kernel(tc, pe, Uq, Uk, out):
                 k_grouped = project(x_mx[0], uk_mx, KEY_ROWS, ())
             if step == KEY_STEP + 1:
                 k_mx = quantise(k_grouped[:, : KEY_ROWS * BANK], keep, "k")
-            if 0 <= step - REQUANTISE_LAG < N_CHUNKS:
-                requantise(step - REQUANTISE_LAG)
             if step < N_CHUNKS:
                 x_mx[step] = quantise(x_grouped[step][:], work, "x")
+            if 0 <= step - REQUANTISE_LAG < N_CHUNKS:
+                requantise(step - REQUANTISE_LAG)
             if step == 0:
                 uk_grouped = regroup_weights(uk_raw, "uk", UK_COLUMNS)
             if step == KEY_STEP - 1:

@@ -18,6 +18,7 @@ CHUNK_ROWS = 4
 CHUNK = CHUNK_ROWS * P
 N_CHUNKS = SQ // CHUNK
 LAST = N_CHUNKS - 1
+N_RESULTS = 2 * N_CHUNKS + 2
 KEY_ROWS = SK // P
 
 PROJECT_LAG = 1
@@ -39,8 +40,8 @@ def tile_multiheadattention_tupe_pa_t_kernel(tc, pe, Uq, Uk, out):
     with ExitStack() as ctx:
         keep = ctx.enter_context(tc.tile_pool(name="keep", bufs=1))
         rows_in = ctx.enter_context(tc.tile_pool(name="rows_in", bufs=N_CHUNKS))
-        work = ctx.enter_context(tc.tile_pool(name="work", bufs=4))
-        rows_out = ctx.enter_context(tc.tile_pool(name="rows_out", bufs=16))
+        work = ctx.enter_context(tc.tile_pool(name="work", bufs=5))
+        rows_out = ctx.enter_context(tc.tile_pool(name="rows_out", bufs=N_RESULTS))
         psum = ctx.enter_context(tc.psum_pool(name="psum", bufs=8))
         ctx.enter_context(tc.manual_schedule())
 

@@ -129,7 +129,7 @@ def tile_multiheadattention_tupe_pa_t_kernel(tc, pe, Uq, Uk, out):
                             identity[:],
                         )
                 empty_bank(
-                    bank == (1 if chunk == 0 else 0),
+                    bank == 0 and chunk > 0,
                     grouped_words[:, bank * BANK : (bank + 1) * BANK].rearrange(
                         "q (w u) -> q w u", u=2
                     ),
@@ -139,10 +139,9 @@ def tile_multiheadattention_tupe_pa_t_kernel(tc, pe, Uq, Uk, out):
 
         def project(x_operand, w_operand, rows, vector_banks):
             w_codes, w_scales = w_operand
-            x_codes, x_scales = x_operand
             grouped = work.tile([P, CHUNK * PACK], BF16, tag="y_grouped", align_bytes=64)
             for bank in range(rows):
-                cols = slice(bank * P, (bank + 1) * P)
+                x_codes, x_scales = x_operand[bank]
                 yt = psum.tile([P, PACK, P], F32, tag="bank")
                 for f in range(PACK):
                     feats = slice(f * P, (f + 1) * P)
@@ -150,8 +149,8 @@ def tile_multiheadattention_tupe_pa_t_kernel(tc, pe, Uq, Uk, out):
                         out=yt[:, f, :],
                         lhsT=w_codes[:, feats].bitcast(FP8X4),
                         lhsT_scale=w_scales[:, feats],
-                        rhs=x_codes[:, cols].bitcast(FP8X4),
-                        rhs_scale=x_scales[:, cols],
+                        rhs=x_codes.bitcast(FP8X4),
+                        rhs_scale=x_scales,
                         start=True,
                         stop=True,
                     )
@@ -164,6 +163,19 @@ def tile_multiheadattention_tupe_pa_t_kernel(tc, pe, Uq, Uk, out):
                 )
             return grouped
 
+        def quantise_rows(grouped, tag, by_halves):
+            parts = 2 if by_halves else 1
+            part_rows = CHUNK_ROWS // parts
+            width = part_rows * P * PACK
+            operands = []
+            for part in range(parts):
+                pool, name = (keep, "%s%d" % (tag, part)) if by_halves else (work, tag)
+                codes, scales = quantise(grouped[:, part * width : (part + 1) * width], pool, name)
+                for r in range(part_rows):
+                    cols = slice(r * P, (r + 1) * P)
+                    operands.append((codes[:, cols], scales[:, cols]))
+            return operands
+
         def project_queries(chunk):
             if chunk == LAST:
                 vector_banks = (0, 2)
@@ -173,21 +185,6 @@ def tile_multiheadattention_tupe_pa_t_kernel(tc, pe, Uq, Uk, out):
                 vector_banks = (0,)
             y_grouped[chunk] = project(x_mx[chunk], uq_mx, CHUNK_ROWS, vector_banks)
 
-        def requantise(chunk):
-            grouped = y_grouped[chunk][:]
-            half = CHUNK * PACK // 2
-            if chunk == LAST:
-                y_mx[chunk] = [
-                    [t[:] for t in quantise(grouped[:, h * half : (h + 1) * half], keep, "q%d" % h)]
-                    for h in range(2)
-                ]
-            else:
-                codes, scales = quantise(grouped, work, "q")
-                width = CHUNK // 2
-                y_mx[chunk] = [
-                    [t[:, h * width : (h + 1) * width] for t in (codes, scales)] for h in range(2)
-                ]
-
         def score(chunk, k_operand):
             k_codes, k_scales = k_operand
             out_rows = chunk_view(out, chunk)
@@ -195,13 +192,11 @@ def tile_multiheadattention_tupe_pa_t_kernel(tc, pe, Uq, Uk, out):
             for bank in range(CHUNK_ROWS // bank_rows):
                 st = psum.tile([P, bank_rows, SK], F32, tag="bank")
                 for i in range(bank_rows):
-                    half, r = divmod(bank * bank_rows + i, 2)
-                    q_codes, q_scales = y_mx[chunk][half]
-                    cols = slice(r * P, (r + 1) * P)
+                    q_codes, q_scales = y_mx[chunk][bank * bank_rows + i]
                     nc.tensor.matmul_mx(
                         out=st[:, i, :],
-                        lhsT=q_codes[:, cols].bitcast(FP8X4),
-                        lhsT_scale=q_scales[:, cols],
+                        lhsT=q_codes.bitcast(FP8X4),
+                        lhsT_scale=q_scales,
                         rhs=k_codes[:].bitcast(FP8X4),
                         rhs_scale=k_scales[:],
                         start=True,
@@ -230,9 +225,10 @@ def tile_multiheadattention_tupe_pa_t_kernel(tc, pe, Uq, Uk, out):
             if step == KEY_STEP + 1:
                 k_mx = quantise(k_grouped[:, : KEY_ROWS * BANK], keep, "k")
             if step < N_CHUNKS:
-                x_mx[step] = quantise(x_grouped[step][:], work, "x")
+                x_mx[step] = quantise_rows(x_grouped[step][:], "x", step == 0)
             if 0 <= step - REQUANTISE_LAG < N_CHUNKS:
-                requantise(step - REQUANTISE_LAG)
+                chunk = step - REQUANTISE_LAG
+                y_mx[chunk] = quantise_rows(y_grouped[chunk][:], "q", chunk == LAST)
             if step == 0:
                 uk_grouped = regroup_weights(uk_raw, "uk", UK_COLUMNS)
             if step == KEY_STEP - 1:

from contextlib import ExitStack

import concourse.masks as masks
import concourse.mybir as mybir

BF16 = mybir.dt.bfloat16
F32 = mybir.dt.float32
U32 = mybir.dt.uint32
U8 = mybir.dt.uint8
FP8X4 = mybir.dt.float8_e4m3fn_x4

P = 128
PACK = 4
SQ, SK, D = 8192, 256, 512
BANK = 512

CHUNK_ROWS = 4
CHUNK = CHUNK_ROWS * P
N_CHUNKS = SQ // CHUNK
LAST = N_CHUNKS - 1
N_RESULTS = 2 * N_CHUNKS + 2
KEY_ROWS = SK // P

PROJECT_LAG = 1
REQUANTISE_LAG = 2
SCORE_LAG = 4

RELIEF = 5

WARM_UP = (5, 2, 1)

UQ_COLUMNS = (0, 80, 48)
UK_COLUMNS = (80, 24, 24)

FLOPS = 2 * D * (SQ * D + SK * D + SQ * SK)


def tile_multiheadattention_tupe_pa_t_kernel(tc, pe, Uq, Uk, out):
    nc = tc.nc
    with ExitStack() as ctx:
        keep = ctx.enter_context(tc.tile_pool(name="keep", bufs=1))
        rows_in = ctx.enter_context(tc.tile_pool(name="rows_in", bufs=N_CHUNKS))
        work = ctx.enter_context(tc.tile_pool(name="work", bufs=5))
        rows_out = ctx.enter_context(tc.tile_pool(name="rows_out", bufs=N_RESULTS))
        psum = ctx.enter_context(tc.psum_pool(name="psum", bufs=8))
        ctx.enter_context(tc.manual_schedule())

        def empty_bank(on_vector, out_ap, in_ap):
            if on_vector:
                nc.vector.tensor_copy(out=out_ap, in_=in_ap)
            else:
                nc.scalar.copy(out=out_ap, in_=in_ap)

        def quantise(grouped, pool, tag):
            width = grouped.shape[1] // PACK
            codes = pool.tile([P, width], U32, tag=tag + "_codes", align_bytes=64)
            scales = pool.tile([P, width], U8, tag=tag + "_scales", align_bytes=64)
            nc.vector.quantize_mx(out=codes[:].bitcast(FP8X4), scales=scales[:], in_=grouped)
            return codes, scales

        def load_weights(w, tag):
            raw = keep.tile([P, PACK, D], BF16, tag=tag + "_raw")
            nc.sync.dma_start(out=raw[:], in_=w.rearrange("(q t) c -> q t c", t=PACK))
            return raw

        def chunk_view(tensor, chunk):
            rows = tensor[chunk * CHUNK : (chunk + 1) * CHUNK, :]
            if chunk == 0:
                return rows.rearrange("(r p) c -> p r c", p=P)
            return rows.rearrange("(p r) c -> p r c", r=CHUNK_ROWS)

        def load_chunk(chunk):
            chunk_rows = rows_in.tile([P, CHUNK_ROWS, D], BF16, tag="chunk_rows")
            view = chunk_view(pe, chunk)
            rows = CHUNK_ROWS // 2 if chunk == 0 else CHUNK_ROWS
            for r in range(0, CHUNK_ROWS, rows):
                nc.sync.dma_start(out=chunk_rows[:, r : r + rows, :], in_=view[:, r : r + rows, :])
            return chunk_rows

        uq_raw = load_weights(Uq, "uq")
        pe_rows = [load_chunk(0), load_chunk(1)]
        uk_raw = load_weights(Uk, "uk")
        for chunk in range(2, N_CHUNKS):
            pe_rows.append(load_chunk(chunk))

        identity = keep.tile([P, P], F32, tag="identity")
        masks.make_identity(nc, identity[:])

        def regroup_weights(raw, tag, columns):
            grouped = keep.tile([P, PACK * D], BF16, tag=tag + "_grouped", align_bytes=64)
            dst = grouped[:].rearrange("q (f m t) -> q m t f", f=PACK, t=PACK)
            src = raw[:].rearrange("q t (m f) -> q m t f", f=PACK)
            a, b = columns[0], columns[0] + columns[1]
            if a:
                nc.gpsimd.tensor_scalar(
                    out=dst[:, :a],
                    in0=src[:, :a],
                    scalar1=1.0,
                    scalar2=0.0,
                    op0=mybir.AluOpType.mult,
                    op1=mybir.AluOpType.add,
                )
            nc.vector.tensor_copy(out=dst[:, a:b], in_=src[:, a:b])
            nc.scalar.copy(out=dst[:, b:], in_=src[:, b:])
            return grouped

        x_grouped, x_mx, y_grouped, y_mx = {}, {}, {}, {}

        zeros = keep.tile([P, BANK], BF16, tag="zeros")
        nc.vector.memset(zeros[:], 0.0)

        def warm_up(count):
            idle = psum.tile([P, BANK], F32, tag="bank")
            for i in range(count):
                nc.tensor.matmul(idle[:], lhsT=zeros[:, :P], rhs=zeros[:], start=True, stop=True)

        def transpose_features(chunk):
            words = pe_rows[chunk][:].rearrange("p r d -> p (r d)").bitcast(F32)
            grouped = work.tile([P, CHUNK * PACK], BF16, tag="x_grouped", align_bytes=64)
            grouped_words = grouped[:].bitcast(F32)
            for bank in range(CHUNK_ROWS // 2):
                xt = psum.tile([P, 2, 2 * P], F32, tag="bank")
                for r in range(2):
                    for u in range(2):
                        row = (2 * bank + r) * 2 * P
                        nc.tensor.transpose(
                            xt[:, u, r * P : (r + 1) * P],
                            words[:, row + u : row + 2 * P : 2],
                            identity[:],
                        )
                empty_bank(
                    bank == 0 and chunk > 0,
                    grouped_words[:, bank * BANK : (bank + 1) * BANK].rearrange(
                        "q (w u) -> q w u", u=2
                    ),
                    xt[:].rearrange("q u w -> q w u"),
                )
            x_grouped[chunk] = grouped

        def project(x_operand, w_operand, rows, vector_banks):
            w_codes, w_scales = w_operand
            grouped = work.tile([P, CHUNK * PACK], BF16, tag="y_grouped", align_bytes=64)
            for bank in range(rows):
                x_codes, x_scales = x_operand[bank]
                yt = psum.tile([P, PACK, P], F32, tag="bank")
                for f in range(PACK):
                    feats = slice(f * P, (f + 1) * P)
                    nc.tensor.matmul_mx(
                        out=yt[:, f, :],
                        lhsT=w_codes[:, feats].bitcast(FP8X4),
                        lhsT_scale=w_scales[:, feats],
                        rhs=x_codes.bitcast(FP8X4),
                        rhs_scale=x_scales,
                        start=True,
                        stop=True,
                    )
                empty_bank(
                    bank in vector_banks,
                    grouped[:, bank * BANK : (bank + 1) * BANK].rearrange(
                        "m (w f) -> m w f", f=PACK
                    ),
                    yt[:].rearrange("m f w -> m w f"),
                )
            return grouped

        def quantise_rows(grouped, tag, by_halves):
            parts = 2 if by_halves else 1
            part_rows = CHUNK_ROWS // parts
            width = part_rows * P * PACK
            operands = []
            for part in range(parts):
                pool, name = (keep, "%s%d" % (tag, part)) if by_halves else (work, tag)
                codes, scales = quantise(grouped[:, part * width : (part + 1) * width], pool, name)
                for r in range(part_rows):
                    cols = slice(r * P, (r + 1) * P)
                    operands.append((codes[:, cols], scales[:, cols]))
            return operands

        def project_queries(chunk):
            if chunk == LAST:
                vector_banks = (0, 2)
            elif chunk % RELIEF == RELIEF - 1:
                vector_banks = ()
            else:
                vector_banks = (0,)
            y_grouped[chunk] = project(x_mx[chunk], uq_mx, CHUNK_ROWS, vector_banks)

        def score(chunk, k_operand):
            k_codes, k_scales = k_operand
            out_rows = chunk_view(out, chunk)
            bank_rows = 1 if chunk == LAST else 2
            for bank in range(CHUNK_ROWS // bank_rows):
                st = psum.tile([P, bank_rows, SK], F32, tag="bank")
                for i in range(bank_rows):
                    q_codes, q_scales = y_mx[chunk][bank * bank_rows + i]
                    nc.tensor.matmul_mx(
                        out=st[:, i, :],
                        lhsT=q_codes.bitcast(FP8X4),
                        lhsT_scale=q_scales,
                        rhs=k_codes[:].bitcast(FP8X4),
                        rhs_scale=k_scales[:],
                        start=True,
                        stop=True,
                    )
                result = rows_out.tile([P, bank_rows, SK], F32, tag="result")
                empty_bank(bank % 2 == 0, result[:], st[:])
                rows = slice(bank * bank_rows, (bank + 1) * bank_rows)
                nc.sync.dma_start(out=out_rows[:, rows, :], in_=result[:])

        KEY_STEP = 1 + PROJECT_LAG
        uq_grouped = regroup_weights(uq_raw, "uq", UQ_COLUMNS)
        uq_mx = quantise(uq_grouped[:], keep, "uq")
        warm_up(WARM_UP[0])
        for step in range(N_CHUNKS + SCORE_LAG):
            if step < N_CHUNKS:
                transpose_features(step)
            if step < 2:
                warm_up(WARM_UP[1 + step])
            if 0 <= step - SCORE_LAG:
                score(step - SCORE_LAG, k_mx)
            if 0 <= step - PROJECT_LAG < N_CHUNKS:
                project_queries(step - PROJECT_LAG)
            if step == KEY_STEP:
                k_grouped = project(x_mx[0], uk_mx, KEY_ROWS, ())
            if step == KEY_STEP + 1:
                k_mx = quantise(k_grouped[:, : KEY_ROWS * BANK], keep, "k")
            if step < N_CHUNKS:
                x_mx[step] = quantise_rows(x_grouped[step][:], "x", step == 0)
            if 0 <= step - REQUANTISE_LAG < N_CHUNKS:
                chunk = step - REQUANTISE_LAG
                y_mx[chunk] = quantise_rows(y_grouped[chunk][:], "q", chunk == LAST)
            if step == 0:
                uk_grouped = regroup_weights(uk_raw, "uk", UK_COLUMNS)
            if step == KEY_STEP - 1:
                uk_mx = quantise(uk_grouped[:], keep, "uk")
